import numpy as np
import ml_dtypes

BF16 = ml_dtypes.bfloat16


def bf(x):
    return np.asarray(x, np.float32).astype(BF16)


def f32(x):
    return np.asarray(x, np.float32)


def f64(x):
    return np.asarray(x).astype(np.float64)


def striped(idx):
    return np.tile(idx.reshape(-1, 16).T, (8, 1))


S, D, M, L, N = 1024, 128, 128, 128, 128
LN_EPS = 1e-6


def setup_inputs():
    return {"table": bf(np.random.standard_normal((S, D))), "w1": bf(np.random.standard_normal((D, M)) / np.sqrt(D)), "b1": f32(0.1 * np.random.standard_normal((M, 1))), "ln_scale": f32(1.0 + 0.1 * np.random.standard_normal((M, 1))), "ln_bias": f32(0.1 * np.random.standard_normal((M, 1))), "w4": bf(np.random.standard_normal((M, L)) / np.sqrt(M)), "b4": f32(0.1 * np.random.standard_normal((L, 1))), "offs": striped(np.random.permutation(np.tile(np.arange(S), 2))[:N])}


def reference(table, w1, b1, ln_scale, ln_bias, w4, b4, offs):
    idx = offs[:16].T.reshape(-1)
    u = f64(w1).T @ f64(table)[idx].T + f64(b1)
    mu = u.mean(axis=0, keepdims=True)
    var = np.square(u - mu).mean(axis=0, keepdims=True)
    h = np.maximum((u - mu) / np.sqrt(var + LN_EPS) * f64(ln_scale) + f64(ln_bias), 0.0)
    return np.exp(f64(w4).T @ h + f64(b4))

@@ -1,0 +1,109 @@
+import concourse.mybir as mybir
+from concourse.masks import make_identity
+
+P = 128
+GENES = 1024
+CELLS = 128
+PIECES = 4
+PIECE_BLOCKS = GENES // P // PIECES
+PIECE_GENES = PIECE_BLOCKS * P
+LN_EPS = 1e-6
+
+FLOPS = 2 * P * P * CELLS + 2 * P * P * CELLS
+BYTES = CELLS * P * 2 + 2 * P * P * 2 + 4 * P * 4 + P * (CELLS // 16) * 2 + P * CELLS * 4
+
+BF16 = mybir.dt.bfloat16
+F32 = mybir.dt.float32
+U16 = mybir.dt.uint16
+ACT = mybir.ActivationFunctionType
+ALU = mybir.AluOpType
+
+
+def tile_gibbsencoder_kernel(tc, table, w1, b1, ln_scale, ln_bias, w4, b4, offs, out):
+    nc = tc.nc
+    with (
+        tc.tile_pool(name="held", bufs=1) as held,
+        tc.psum_pool(name="flip", bufs=PIECES) as flip,
+        tc.psum_pool(name="chain", bufs=1) as chain,
+    ):
+        table_blocks = table.rearrange("(b p) d -> p b d", p=P)
+        rows = []
+        for piece in range(PIECES):
+            rows_piece = held.tile([P, PIECE_BLOCKS, P], BF16, name=f"rows{piece}")
+            queue = nc.sync if piece % 2 == 0 else nc.scalar
+            queue.dma_start(
+                rows_piece[:],
+                table_blocks[:, piece * PIECE_BLOCKS : (piece + 1) * PIECE_BLOCKS, :],
+            )
+            rows.append(rows_piece)
+        offsets = held.tile([P, CELLS // 16], U16, name="offsets")
+        nc.sync.dma_start(offsets[:], offs)
+        w1_sb = held.tile([P, P], BF16, name="w1_sb")
+        nc.sync.dma_start(w1_sb[:], w1)
+        w4_sb = held.tile([P, P], BF16, name="w4_sb")
+        nc.scalar.dma_start(w4_sb[:], w4)
+
+        ident_bf = held.tile([P, P], BF16, name="ident_bf")
+        make_identity(nc, ident_bf[:])
+        ident_f32 = held.tile([P, P], F32, name="ident_f32")
+        make_identity(nc, ident_f32[:])
+        eps = held.tile([P, 1], F32, name="eps")
+        nc.vector.memset(eps[:], LN_EPS)
+        warm = held.tile([P, 1], F32, name="warm")
+        nc.scalar.activation(warm[:], eps[:], ACT.Sqrt)
+
+        b1_sb = held.tile([P, 1], F32, name="b1_sb")
+        scale_sb = held.tile([P, 1], F32, name="scale_sb")
+        bias_sb = held.tile([P, 1], F32, name="bias_sb")
+        b4_sb = held.tile([P, 1], F32, name="b4_sb")
+        with nc.allow_non_contiguous_dma(reason="one float to a partition"):
+            nc.gpsimd.dma_start(b1_sb[:], b1)
+            nc.gpsimd.dma_start(scale_sb[:], ln_scale)
+            nc.gpsimd.dma_start(bias_sb[:], ln_bias)
+            nc.gpsimd.dma_start(b4_sb[:], b4)
+
+        window = held.tile([P, GENES], BF16, name="window")
+        for piece in range(PIECES):
+            flipped = flip.tile([P, PIECE_GENES], BF16, name="flipped")
+            for block in range(PIECE_BLOCKS):
+                nc.tensor.transpose(
+                    flipped[:, block * P : (block + 1) * P], rows[piece][:, block, :], ident_bf[:]
+                )
+            window_part = window[:, piece * PIECE_GENES : (piece + 1) * PIECE_GENES]
+            if piece % 2 == 0:
+                nc.vector.tensor_copy(window_part, flipped[:])
+            else:
+                nc.scalar.copy(window_part, flipped[:])
+
+        u_ps = chain.tile([P, CELLS], F32, name="u_ps")
+        nc.tensor.matmul(u_ps[:], w1_sb[:], window[:].indirect(offsets[:]), start=True, stop=True)
+        u_sb = held.tile([P, CELLS], F32, name="u_sb")
+        nc.vector.tensor_scalar_add(u_sb[:], u_ps[:], b1_sb[:])
+
+        ut_ps = chain.tile([CELLS, P], F32, name="ut_ps")
+        nc.tensor.transpose(ut_ps[:], u_sb[:], ident_f32[:])
+        stats = held.tile([CELLS, 6], F32, name="stats")
+        nc.vector.bn_stats(stats[:], ut_ps[:])
+        mean_var = held.tile([CELLS, 2], F32, name="mean_var")
+        nc.vector.bn_aggr(mean_var[:], stats[:])
+        std = held.tile([CELLS, 1], F32, name="std")
+        nc.scalar.activation(std[:], mean_var[:, 1:2], ACT.Sqrt, bias=eps[:])
+        rstd = held.tile([CELLS, 1], F32, name="rstd")
+        nc.vector.reciprocal(rstd[:], std[:])
+        zt_sb = held.tile([CELLS, P], F32, name="zt_sb")
+        nc.vector.tensor_scalar(
+            zt_sb[:], ut_ps[:], mean_var[:, 0:1], rstd[:], ALU.subtract, ALU.mult
+        )
+        z_ps = chain.tile([P, CELLS], F32, name="z_ps")
+        nc.tensor.transpose(z_ps[:], zt_sb[:], ident_f32[:])
+
+        affine = held.tile([P, CELLS], F32, name="affine")
+        nc.vector.tensor_scalar(affine[:], z_ps[:], scale_sb[:], bias_sb[:], ALU.mult, ALU.add)
+        h = held.tile([P, CELLS], BF16, name="h")
+        nc.vector.tensor_scalar_max(h[:], affine[:], 0.0)
+
+        o_ps = chain.tile([P, CELLS], F32, name="o_ps")
+        nc.tensor.matmul(o_ps[:], w4_sb[:], h[:], start=True, stop=True)
+        result = held.tile([P, CELLS], F32, name="result")
+        nc.scalar.activation(result[:], o_ps[:], ACT.Exp, bias=b4_sb[:])
+        nc.sync.dma_start(out, result[:])

@@ -57,10 +57,10 @@ def tile_gibbsencoder_kernel(tc, table, w1, b1, ln_scale, ln_bias, w4, b4, offs,
         bias_sb = held.tile([P, 1], F32, name="bias_sb")
         b4_sb = held.tile([P, 1], F32, name="b4_sb")
         with nc.allow_non_contiguous_dma(reason="one float to a partition"):
-            nc.gpsimd.dma_start(b1_sb[:], b1)
-            nc.gpsimd.dma_start(scale_sb[:], ln_scale)
-            nc.gpsimd.dma_start(bias_sb[:], ln_bias)
-            nc.gpsimd.dma_start(b4_sb[:], b4)
+            nc.sync.dma_start(b1_sb[:], b1)
+            nc.scalar.dma_start(scale_sb[:], ln_scale)
+            nc.sync.dma_start(bias_sb[:], ln_bias)
+            nc.scalar.dma_start(b4_sb[:], b4)
 
         window = held.tile([P, GENES], BF16, name="window")
         for piece in range(PIECES):

@@ -8,6 +8,8 @@ PIECES = 4
 PIECE_BLOCKS = GENES // P // PIECES
 PIECE_GENES = PIECE_BLOCKS * P
 LN_EPS = 1e-6
+BANK_F32 = 512
+WARM_MATMULS = 4
 
 FLOPS = 2 * P * P * CELLS + 2 * P * P * CELLS
 BYTES = CELLS * P * 2 + 2 * P * P * 2 + 4 * P * 4 + P * (CELLS // 16) * 2 + P * CELLS * 4
@@ -42,6 +44,12 @@ def tile_gibbsencoder_kernel(tc, table, w1, b1, ln_scale, ln_bias, w4, b4, offs,
         nc.sync.dma_start(w1_sb[:], w1)
         w4_sb = held.tile([P, P], BF16, name="w4_sb")
         nc.scalar.dma_start(w4_sb[:], w4)
+
+        zeros = held.tile([P, BANK_F32], BF16, name="zeros")
+        nc.vector.memset(zeros[:], 0.0)
+        warm_ps = chain.tile([P, BANK_F32], F32, name="warm_ps", tag="first_and_last")
+        for repeat in range(WARM_MATMULS):
+            nc.tensor.matmul(warm_ps[:], zeros[:, 0:P], zeros[:], start=True, stop=True)
 
         ident_bf = held.tile([P, P], BF16, name="ident_bf")
         make_identity(nc, ident_bf[:])
@@ -102,7 +110,7 @@ def tile_gibbsencoder_kernel(tc, table, w1, b1, ln_scale, ln_bias, w4, b4, offs,
         h = held.tile([P, CELLS], BF16, name="h")
         nc.vector.tensor_scalar_max(h[:], affine[:], 0.0)
 
-        o_ps = chain.tile([P, CELLS], F32, name="o_ps")
+        o_ps = chain.tile([P, CELLS], F32, name="o_ps", tag="first_and_last")
         nc.tensor.matmul(o_ps[:], w4_sb[:], h[:], start=True, stop=True)
         result = held.tile([P, CELLS], F32, name="result")
         nc.scalar.activation(result[:], o_ps[:], ACT.Exp, bias=b4_sb[:])

@@ -8,8 +8,6 @@ PIECES = 4
 PIECE_BLOCKS = GENES // P // PIECES
 PIECE_GENES = PIECE_BLOCKS * P
 LN_EPS = 1e-6
-BANK_F32 = 512
-WARM_MATMULS = 4
 
 FLOPS = 2 * P * P * CELLS + 2 * P * P * CELLS
 BYTES = CELLS * P * 2 + 2 * P * P * 2 + 4 * P * 4 + P * (CELLS // 16) * 2 + P * CELLS * 4
@@ -45,12 +43,6 @@ def tile_gibbsencoder_kernel(tc, table, w1, b1, ln_scale, ln_bias, w4, b4, offs,
         w4_sb = held.tile([P, P], BF16, name="w4_sb")
         nc.scalar.dma_start(w4_sb[:], w4)
 
-        zeros = held.tile([P, BANK_F32], BF16, name="zeros")
-        nc.vector.memset(zeros[:], 0.0)
-        warm_ps = chain.tile([P, BANK_F32], F32, name="warm_ps", tag="first_and_last")
-        for repeat in range(WARM_MATMULS):
-            nc.tensor.matmul(warm_ps[:], zeros[:, 0:P], zeros[:], start=True, stop=True)
-
         ident_bf = held.tile([P, P], BF16, name="ident_bf")
         make_identity(nc, ident_bf[:])
         ident_f32 = held.tile([P, P], F32, name="ident_f32")
@@ -79,9 +71,9 @@ def tile_gibbsencoder_kernel(tc, table, w1, b1, ln_scale, ln_bias, w4, b4, offs,
                 )
             window_part = window[:, piece * PIECE_GENES : (piece + 1) * PIECE_GENES]
             if piece % 2 == 0:
-                nc.vector.tensor_copy(window_part, flipped[:])
-            else:
                 nc.scalar.copy(window_part, flipped[:])
+            else:
+                nc.vector.tensor_copy(window_part, flipped[:])
 
         u_ps = chain.tile([P, CELLS], F32, name="u_ps")
         nc.tensor.matmul(u_ps[:], w1_sb[:], window[:].indirect(offsets[:]), start=True, stop=True)
@@ -110,7 +102,7 @@ def tile_gibbsencoder_kernel(tc, table, w1, b1, ln_scale, ln_bias, w4, b4, offs,
         h = held.tile([P, CELLS], BF16, name="h")
         nc.vector.tensor_scalar_max(h[:], affine[:], 0.0)
 
-        o_ps = chain.tile([P, CELLS], F32, name="o_ps", tag="first_and_last")
+        o_ps = chain.tile([P, CELLS], F32, name="o_ps")
         nc.tensor.matmul(o_ps[:], w4_sb[:], h[:], start=True, stop=True)
         result = held.tile([P, CELLS], F32, name="result")
         nc.scalar.activation(result[:], o_ps[:], ACT.Exp, bias=b4_sb[:])

@@ -53,12 +53,12 @@ def tile_gibbsencoder_kernel(tc, table, w1, b1, ln_scale, ln_bias, w4, b4, offs,
         nc.scalar.activation(warm[:], eps[:], ACT.Sqrt)
 
         b1_sb = held.tile([P, 1], F32, name="b1_sb")
-        scale_sb = held.tile([P, 1], F32, name="scale_sb")
+        scale_bc = held.tile([CELLS, P], F32, name="scale_bc")
         bias_sb = held.tile([P, 1], F32, name="bias_sb")
         b4_sb = held.tile([P, 1], F32, name="b4_sb")
         with nc.allow_non_contiguous_dma(reason="one float to a partition"):
             nc.sync.dma_start(b1_sb[:], b1)
-            nc.scalar.dma_start(scale_sb[:], ln_scale)
+            nc.scalar.dma_start(scale_bc[:], ln_scale.rearrange("m o -> (m o)").partition_broadcast(CELLS))
             nc.sync.dma_start(bias_sb[:], ln_bias)
             nc.scalar.dma_start(b4_sb[:], b4)
 
@@ -71,9 +71,9 @@ def tile_gibbsencoder_kernel(tc, table, w1, b1, ln_scale, ln_bias, w4, b4, offs,
                 )
             window_part = window[:, piece * PIECE_GENES : (piece + 1) * PIECE_GENES]
             if piece % 2 == 0:
-                nc.scalar.copy(window_part, flipped[:])
-            else:
                 nc.vector.tensor_copy(window_part, flipped[:])
+            else:
+                nc.scalar.copy(window_part, flipped[:])
 
         u_ps = chain.tile([P, CELLS], F32, name="u_ps")
         nc.tensor.matmul(u_ps[:], w1_sb[:], window[:].indirect(offsets[:]), start=True, stop=True)
@@ -88,19 +88,19 @@ def tile_gibbsencoder_kernel(tc, table, w1, b1, ln_scale, ln_bias, w4, b4, offs,
         nc.vector.bn_aggr(mean_var[:], stats[:])
         std = held.tile([CELLS, 1], F32, name="std")
         nc.scalar.activation(std[:], mean_var[:, 1:2], ACT.Sqrt, bias=eps[:])
+        centred = held.tile([CELLS, P], F32, name="centred")
+        nc.vector.scalar_tensor_tensor(
+            centred[:], ut_ps[:], mean_var[:, 0:1], scale_bc[:], ALU.subtract, ALU.mult
+        )
         rstd = held.tile([CELLS, 1], F32, name="rstd")
         nc.vector.reciprocal(rstd[:], std[:])
         zt_sb = held.tile([CELLS, P], F32, name="zt_sb")
-        nc.vector.tensor_scalar(
-            zt_sb[:], ut_ps[:], mean_var[:, 0:1], rstd[:], ALU.subtract, ALU.mult
-        )
+        nc.vector.tensor_scalar_mul(zt_sb[:], centred[:], rstd[:])
         z_ps = chain.tile([P, CELLS], F32, name="z_ps")
         nc.tensor.transpose(z_ps[:], zt_sb[:], ident_f32[:])
 
-        affine = held.tile([P, CELLS], F32, name="affine")
-        nc.vector.tensor_scalar(affine[:], z_ps[:], scale_sb[:], bias_sb[:], ALU.mult, ALU.add)
         h = held.tile([P, CELLS], BF16, name="h")
-        nc.vector.tensor_scalar_max(h[:], affine[:], 0.0)
+        nc.vector.tensor_scalar(h[:], z_ps[:], bias_sb[:], 0.0, ALU.add, ALU.max)
 
         o_ps = chain.tile([P, CELLS], F32, name="o_ps")
         nc.tensor.matmul(o_ps[:], w4_sb[:], h[:], start=True, stop=True)

@@ -47,10 +47,8 @@ def tile_gibbsencoder_kernel(tc, table, w1, b1, ln_scale, ln_bias, w4, b4, offs,
         make_identity(nc, ident_bf[:])
         ident_f32 = held.tile([P, P], F32, name="ident_f32")
         make_identity(nc, ident_f32[:])
-        eps = held.tile([P, 1], F32, name="eps")
-        nc.vector.memset(eps[:], LN_EPS)
-        warm = held.tile([P, 1], F32, name="warm")
-        nc.scalar.activation(warm[:], eps[:], ACT.Sqrt)
+        neg_half = held.tile([CELLS, 1], F32, name="neg_half")
+        nc.vector.memset(neg_half[:], -0.5)
 
         b1_sb = held.tile([P, 1], F32, name="b1_sb")
         scale_bc = held.tile([CELLS, P], F32, name="scale_bc")
@@ -86,14 +84,14 @@ def tile_gibbsencoder_kernel(tc, table, w1, b1, ln_scale, ln_bias, w4, b4, offs,
         nc.vector.bn_stats(stats[:], ut_ps[:])
         mean_var = held.tile([CELLS, 2], F32, name="mean_var")
         nc.vector.bn_aggr(mean_var[:], stats[:])
-        std = held.tile([CELLS, 1], F32, name="std")
-        nc.scalar.activation(std[:], mean_var[:, 1:2], ACT.Sqrt, bias=eps[:])
+        var_eps = held.tile([CELLS, 1], F32, name="var_eps")
+        nc.vector.tensor_scalar_add(var_eps[:], mean_var[:, 1:2], LN_EPS)
+        rstd = held.tile([CELLS, 1], F32, name="rstd")
+        nc.gpsimd.tensor_tensor(rstd[:], var_eps[:], neg_half[:], ALU.pow)
         centred = held.tile([CELLS, P], F32, name="centred")
         nc.vector.scalar_tensor_tensor(
             centred[:], ut_ps[:], mean_var[:, 0:1], scale_bc[:], ALU.subtract, ALU.mult
         )
-        rstd = held.tile([CELLS, 1], F32, name="rstd")
-        nc.vector.reciprocal(rstd[:], std[:])
         zt_sb = held.tile([CELLS, P], F32, name="zt_sb")
         nc.vector.tensor_scalar_mul(zt_sb[:], centred[:], rstd[:])
         z_ps = chain.tile([P, CELLS], F32, name="z_ps")

@@ -8,6 +8,8 @@ PIECES = 4
 PIECE_BLOCKS = GENES // P // PIECES
 PIECE_GENES = PIECE_BLOCKS * P
 LN_EPS = 1e-6
+WARM_MATMULS = 4
+WARM_REPEATS = 4
 
 FLOPS = 2 * P * P * CELLS + 2 * P * P * CELLS
 BYTES = CELLS * P * 2 + 2 * P * P * 2 + 4 * P * 4 + P * (CELLS // 16) * 2 + P * CELLS * 4
@@ -43,20 +45,34 @@ def tile_gibbsencoder_kernel(tc, table, w1, b1, ln_scale, ln_bias, w4, b4, offs,
         w4_sb = held.tile([P, P], BF16, name="w4_sb")
         nc.scalar.dma_start(w4_sb[:], w4)
 
+        zeros = held.tile([P, P], BF16, name="zeros")
+        nc.vector.memset(zeros[:], 0.0)
+        warm_ps = chain.tile([P, WARM_REPEATS, P], F32, name="warm_ps", tag="first_and_last")
+        for repeat in range(WARM_MATMULS):
+            nc.tensor.matmul(
+                warm_ps[:],
+                zeros[:],
+                zeros[:].unsqueeze(1).to_broadcast([P, WARM_REPEATS, P]),
+                start=True,
+                stop=True,
+            )
+
         ident_bf = held.tile([P, P], BF16, name="ident_bf")
         make_identity(nc, ident_bf[:])
         ident_f32 = held.tile([P, P], F32, name="ident_f32")
         make_identity(nc, ident_f32[:])
-        neg_half = held.tile([CELLS, 1], F32, name="neg_half")
-        nc.vector.memset(neg_half[:], -0.5)
+        eps = held.tile([P, 1], F32, name="eps")
+        nc.vector.memset(eps[:], LN_EPS)
+        warm = held.tile([P, 1], F32, name="warm")
+        nc.scalar.activation(warm[:], eps[:], ACT.Sqrt)
 
         b1_sb = held.tile([P, 1], F32, name="b1_sb")
-        scale_bc = held.tile([CELLS, P], F32, name="scale_bc")
+        scale_sb = held.tile([P, 1], F32, name="scale_sb")
         bias_sb = held.tile([P, 1], F32, name="bias_sb")
         b4_sb = held.tile([P, 1], F32, name="b4_sb")
         with nc.allow_non_contiguous_dma(reason="one float to a partition"):
             nc.sync.dma_start(b1_sb[:], b1)
-            nc.scalar.dma_start(scale_bc[:], ln_scale.rearrange("m o -> (m o)").partition_broadcast(CELLS))
+            nc.scalar.dma_start(scale_sb[:], ln_scale)
             nc.sync.dma_start(bias_sb[:], ln_bias)
             nc.scalar.dma_start(b4_sb[:], b4)
 
@@ -84,23 +100,23 @@ def tile_gibbsencoder_kernel(tc, table, w1, b1, ln_scale, ln_bias, w4, b4, offs,
         nc.vector.bn_stats(stats[:], ut_ps[:])
         mean_var = held.tile([CELLS, 2], F32, name="mean_var")
         nc.vector.bn_aggr(mean_var[:], stats[:])
-        var_eps = held.tile([CELLS, 1], F32, name="var_eps")
-        nc.vector.tensor_scalar_add(var_eps[:], mean_var[:, 1:2], LN_EPS)
+        std = held.tile([CELLS, 1], F32, name="std")
+        nc.scalar.activation(std[:], mean_var[:, 1:2], ACT.Sqrt, bias=eps[:])
         rstd = held.tile([CELLS, 1], F32, name="rstd")
-        nc.gpsimd.tensor_tensor(rstd[:], var_eps[:], neg_half[:], ALU.pow)
-        centred = held.tile([CELLS, P], F32, name="centred")
-        nc.vector.scalar_tensor_tensor(
-            centred[:], ut_ps[:], mean_var[:, 0:1], scale_bc[:], ALU.subtract, ALU.mult
-        )
+        nc.vector.reciprocal(rstd[:], std[:])
         zt_sb = held.tile([CELLS, P], F32, name="zt_sb")
-        nc.vector.tensor_scalar_mul(zt_sb[:], centred[:], rstd[:])
+        nc.vector.tensor_scalar(
+            zt_sb[:], ut_ps[:], mean_var[:, 0:1], rstd[:], ALU.subtract, ALU.mult
+        )
         z_ps = chain.tile([P, CELLS], F32, name="z_ps")
         nc.tensor.transpose(z_ps[:], zt_sb[:], ident_f32[:])
 
+        affine = held.tile([P, CELLS], F32, name="affine")
+        nc.vector.tensor_scalar(affine[:], z_ps[:], scale_sb[:], bias_sb[:], ALU.mult, ALU.add)
         h = held.tile([P, CELLS], BF16, name="h")
-        nc.vector.tensor_scalar(h[:], z_ps[:], bias_sb[:], 0.0, ALU.add, ALU.max)
+        nc.vector.tensor_scalar_max(h[:], affine[:], 0.0)
 
-        o_ps = chain.tile([P, CELLS], F32, name="o_ps")
+        o_ps = chain.tile([P, CELLS], F32, name="o_ps", tag="first_and_last")
         nc.tensor.matmul(o_ps[:], w4_sb[:], h[:], start=True, stop=True)
         result = held.tile([P, CELLS], F32, name="result")
         nc.scalar.activation(result[:], o_ps[:], ACT.Exp, bias=b4_sb[:])

@@ -8,8 +8,6 @@ PIECES = 4
 PIECE_BLOCKS = GENES // P // PIECES
 PIECE_GENES = PIECE_BLOCKS * P
 LN_EPS = 1e-6
-WARM_MATMULS = 4
-WARM_REPEATS = 4
 
 FLOPS = 2 * P * P * CELLS + 2 * P * P * CELLS
 BYTES = CELLS * P * 2 + 2 * P * P * 2 + 4 * P * 4 + P * (CELLS // 16) * 2 + P * CELLS * 4
@@ -32,8 +30,7 @@ def tile_gibbsencoder_kernel(tc, table, w1, b1, ln_scale, ln_bias, w4, b4, offs,
         rows = []
         for piece in range(PIECES):
             rows_piece = held.tile([P, PIECE_BLOCKS, P], BF16, name=f"rows{piece}")
-            queue = nc.sync if piece % 2 == 0 else nc.scalar
-            queue.dma_start(
+            nc.sync.dma_start(
                 rows_piece[:],
                 table_blocks[:, piece * PIECE_BLOCKS : (piece + 1) * PIECE_BLOCKS, :],
             )
@@ -43,19 +40,6 @@ def tile_gibbsencoder_kernel(tc, table, w1, b1, ln_scale, ln_bias, w4, b4, offs,
         w1_sb = held.tile([P, P], BF16, name="w1_sb")
         nc.sync.dma_start(w1_sb[:], w1)
         w4_sb = held.tile([P, P], BF16, name="w4_sb")
-        nc.scalar.dma_start(w4_sb[:], w4)
-
-        zeros = held.tile([P, P], BF16, name="zeros")
-        nc.vector.memset(zeros[:], 0.0)
-        warm_ps = chain.tile([P, WARM_REPEATS, P], F32, name="warm_ps", tag="first_and_last")
-        for repeat in range(WARM_MATMULS):
-            nc.tensor.matmul(
-                warm_ps[:],
-                zeros[:],
-                zeros[:].unsqueeze(1).to_broadcast([P, WARM_REPEATS, P]),
-                start=True,
-                stop=True,
-            )
 
         ident_bf = held.tile([P, P], BF16, name="ident_bf")
         make_identity(nc, ident_bf[:])
@@ -72,9 +56,10 @@ def tile_gibbsencoder_kernel(tc, table, w1, b1, ln_scale, ln_bias, w4, b4, offs,
         b4_sb = held.tile([P, 1], F32, name="b4_sb")
         with nc.allow_non_contiguous_dma(reason="one float to a partition"):
             nc.sync.dma_start(b1_sb[:], b1)
-            nc.scalar.dma_start(scale_sb[:], ln_scale)
+            nc.sync.dma_start(scale_sb[:], ln_scale)
             nc.sync.dma_start(bias_sb[:], ln_bias)
-            nc.scalar.dma_start(b4_sb[:], b4)
+            nc.sync.dma_start(w4_sb[:], w4)
+            nc.sync.dma_start(b4_sb[:], b4)
 
         window = held.tile([P, GENES], BF16, name="window")
         for piece in range(PIECES):
@@ -116,7 +101,7 @@ def tile_gibbsencoder_kernel(tc, table, w1, b1, ln_scale, ln_bias, w4, b4, offs,
         h = held.tile([P, CELLS], BF16, name="h")
         nc.vector.tensor_scalar_max(h[:], affine[:], 0.0)
 
-        o_ps = chain.tile([P, CELLS], F32, name="o_ps", tag="first_and_last")
+        o_ps = chain.tile([P, CELLS], F32, name="o_ps")
         nc.tensor.matmul(o_ps[:], w4_sb[:], h[:], start=True, stop=True)
         result = held.tile([P, CELLS], F32, name="result")
         nc.scalar.activation(result[:], o_ps[:], ACT.Exp, bias=b4_sb[:])

@@ -26,6 +26,11 @@ def tile_gibbsencoder_kernel(tc, table, w1, b1, ln_scale, ln_bias, w4, b4, offs,
         tc.psum_pool(name="flip", bufs=PIECES) as flip,
         tc.psum_pool(name="chain", bufs=1) as chain,
     ):
+        b1_sb = held.tile([P, 1], F32, name="b1_sb")
+        with nc.allow_non_contiguous_dma(reason="one float to a partition"):
+            nc.sync.dma_start(b1_sb[:], b1)
+        w1_sb = held.tile([P, P], BF16, name="w1_sb")
+        nc.sync.dma_start(w1_sb[:], w1)
         table_blocks = table.rearrange("(b p) d -> p b d", p=P)
         rows = []
         for piece in range(PIECES):
@@ -37,29 +42,38 @@ def tile_gibbsencoder_kernel(tc, table, w1, b1, ln_scale, ln_bias, w4, b4, offs,
             rows.append(rows_piece)
         offsets = held.tile([P, CELLS // 16], U16, name="offsets")
         nc.sync.dma_start(offsets[:], offs)
-        w1_sb = held.tile([P, P], BF16, name="w1_sb")
-        nc.sync.dma_start(w1_sb[:], w1)
-        w4_sb = held.tile([P, P], BF16, name="w4_sb")
-
-        ident_bf = held.tile([P, P], BF16, name="ident_bf")
-        make_identity(nc, ident_bf[:])
-        ident_f32 = held.tile([P, P], F32, name="ident_f32")
-        make_identity(nc, ident_f32[:])
-        eps = held.tile([P, 1], F32, name="eps")
-        nc.vector.memset(eps[:], LN_EPS)
-        warm = held.tile([P, 1], F32, name="warm")
-        nc.scalar.activation(warm[:], eps[:], ACT.Sqrt)
-
-        b1_sb = held.tile([P, 1], F32, name="b1_sb")
         scale_sb = held.tile([P, 1], F32, name="scale_sb")
         bias_sb = held.tile([P, 1], F32, name="bias_sb")
+        w4_sb = held.tile([P, P], BF16, name="w4_sb")
         b4_sb = held.tile([P, 1], F32, name="b4_sb")
         with nc.allow_non_contiguous_dma(reason="one float to a partition"):
-            nc.sync.dma_start(b1_sb[:], b1)
             nc.sync.dma_start(scale_sb[:], ln_scale)
             nc.sync.dma_start(bias_sb[:], ln_bias)
             nc.sync.dma_start(w4_sb[:], w4)
             nc.sync.dma_start(b4_sb[:], b4)
+
+        ident_bf = held.tile([P, P], BF16, name="ident_bf")
+        make_identity(nc, ident_bf[:])
+        mean_weights = held.tile([P, P], F32, name="mean_weights")
+        nc.vector.memset(mean_weights[:], 1.0 / P)
+        eps = held.tile([P, 1], F32, name="eps")
+        nc.vector.memset(eps[:], LN_EPS)
+        warm = held.tile([P, 1], F32, name="warm")
+        nc.scalar.activation(warm[:], eps[:], ACT.Abs_reciprocal_sqrt)
+
+        b1_mean_ps = chain.tile([P, 1], F32, name="b1_mean_ps")
+        nc.tensor.matmul(b1_mean_ps[:], mean_weights[:], b1_sb[:], start=True, stop=True)
+        b1c = held.tile([P, 1], F32, name="b1c")
+        nc.vector.tensor_tensor(b1c[:], b1_sb[:], b1_mean_ps[:], ALU.subtract)
+        w1_over_p = held.tile([P, P], F32, name="w1_over_p")
+        w1_mean = held.tile([P, 1], F32, name="w1_mean")
+        nc.scalar.activation(w1_over_p[:], w1_sb[:], ACT.Copy, scale=1.0 / P, accum_out=w1_mean[:])
+        w1c_hi = held.tile([P, P], BF16, name="w1c_hi")
+        nc.vector.tensor_scalar_sub(w1c_hi[:], w1_sb[:], w1_mean[:])
+        w1c_lo = held.tile([P, P], BF16, name="w1c_lo")
+        nc.vector.scalar_tensor_tensor(
+            w1c_lo[:], w1_sb[:], w1_mean[:], w1c_hi[:], ALU.subtract, ALU.subtract
+        )
 
         window = held.tile([P, GENES], BF16, name="window")
         for piece in range(PIECES):
@@ -74,32 +88,23 @@ def tile_gibbsencoder_kernel(tc, table, w1, b1, ln_scale, ln_bias, w4, b4, offs,
             else:
                 nc.scalar.copy(window_part, flipped[:])
 
-        u_ps = chain.tile([P, CELLS], F32, name="u_ps")
-        nc.tensor.matmul(u_ps[:], w1_sb[:], window[:].indirect(offsets[:]), start=True, stop=True)
-        u_sb = held.tile([P, CELLS], F32, name="u_sb")
-        nc.vector.tensor_scalar_add(u_sb[:], u_ps[:], b1_sb[:])
+        uc_ps = chain.tile([P, CELLS], F32, name="uc_ps")
+        nc.tensor.matmul(uc_ps[:], w1c_hi[:], window[:].indirect(offsets[:]), start=True, stop=False)
+        nc.tensor.matmul(uc_ps[:], w1c_lo[:], window[:].indirect(offsets[:]), start=False, stop=True)
 
-        ut_ps = chain.tile([CELLS, P], F32, name="ut_ps")
-        nc.tensor.transpose(ut_ps[:], u_sb[:], ident_f32[:])
-        stats = held.tile([CELLS, 6], F32, name="stats")
-        nc.vector.bn_stats(stats[:], ut_ps[:])
-        mean_var = held.tile([CELLS, 2], F32, name="mean_var")
-        nc.vector.bn_aggr(mean_var[:], stats[:])
-        std = held.tile([CELLS, 1], F32, name="std")
-        nc.scalar.activation(std[:], mean_var[:, 1:2], ACT.Sqrt, bias=eps[:])
-        rstd = held.tile([CELLS, 1], F32, name="rstd")
-        nc.vector.reciprocal(rstd[:], std[:])
-        zt_sb = held.tile([CELLS, P], F32, name="zt_sb")
-        nc.vector.tensor_scalar(
-            zt_sb[:], ut_ps[:], mean_var[:, 0:1], rstd[:], ALU.subtract, ALU.mult
-        )
-        z_ps = chain.tile([P, CELLS], F32, name="z_ps")
-        nc.tensor.transpose(z_ps[:], zt_sb[:], ident_f32[:])
+        squares = held.tile([P, CELLS], F32, name="squares")
+        nc.scalar.activation(squares[:], uc_ps[:], ACT.Square, bias=b1c[:])
+        var_ps = chain.tile([P, CELLS], F32, name="var_ps")
+        nc.tensor.matmul(var_ps[:], mean_weights[:], squares[:], start=True, stop=True)
+        gained = held.tile([P, CELLS], F32, name="gained")
+        nc.vector.tensor_scalar(gained[:], uc_ps[:], b1c[:], scale_sb[:], ALU.add, ALU.mult)
+        rstd = held.tile([P, CELLS], F32, name="rstd")
+        nc.scalar.activation(rstd[:], var_ps[:], ACT.Abs_reciprocal_sqrt, bias=eps[:])
 
-        affine = held.tile([P, CELLS], F32, name="affine")
-        nc.vector.tensor_scalar(affine[:], z_ps[:], scale_sb[:], bias_sb[:], ALU.mult, ALU.add)
+        normed = held.tile([P, CELLS], F32, name="normed")
+        nc.vector.tensor_tensor(normed[:], gained[:], rstd[:], ALU.mult)
         h = held.tile([P, CELLS], BF16, name="h")
-        nc.vector.tensor_scalar_max(h[:], affine[:], 0.0)
+        nc.vector.tensor_scalar(h[:], normed[:], bias_sb[:], 0.0, ALU.add, ALU.max)
 
         o_ps = chain.tile([P, CELLS], F32, name="o_ps")
         nc.tensor.matmul(o_ps[:], w4_sb[:], h[:], start=True, stop=True)

@@ -28,9 +28,9 @@ def tile_gibbsencoder_kernel(tc, table, w1, b1, ln_scale, ln_bias, w4, b4, offs,
     ):
         b1_sb = held.tile([P, 1], F32, name="b1_sb")
         with nc.allow_non_contiguous_dma(reason="one float to a partition"):
-            nc.sync.dma_start(b1_sb[:], b1)
+            nc.scalar.dma_start(b1_sb[:], b1)
         w1_sb = held.tile([P, P], BF16, name="w1_sb")
-        nc.sync.dma_start(w1_sb[:], w1)
+        nc.scalar.dma_start(w1_sb[:], w1)
         table_blocks = table.rearrange("(b p) d -> p b d", p=P)
         rows = []
         for piece in range(PIECES):

import concourse.mybir as mybir
from concourse.masks import make_identity

P = 128
GENES = 1024
CELLS = 128
PIECES = 4
PIECE_BLOCKS = GENES // P // PIECES
PIECE_GENES = PIECE_BLOCKS * P
LN_EPS = 1e-6

FLOPS = 2 * P * P * CELLS + 2 * P * P * CELLS
BYTES = CELLS * P * 2 + 2 * P * P * 2 + 4 * P * 4 + P * (CELLS // 16) * 2 + P * CELLS * 4

BF16 = mybir.dt.bfloat16
F32 = mybir.dt.float32
U16 = mybir.dt.uint16
ACT = mybir.ActivationFunctionType
ALU = mybir.AluOpType


def tile_gibbsencoder_kernel(tc, table, w1, b1, ln_scale, ln_bias, w4, b4, offs, out):
    nc = tc.nc
    with (
        tc.tile_pool(name="held", bufs=1) as held,
        tc.psum_pool(name="flip", bufs=PIECES) as flip,
        tc.psum_pool(name="chain", bufs=1) as chain,
    ):
        b1_sb = held.tile([P, 1], F32, name="b1_sb")
        with nc.allow_non_contiguous_dma(reason="one float to a partition"):
            nc.scalar.dma_start(b1_sb[:], b1)
        w1_sb = held.tile([P, P], BF16, name="w1_sb")
        nc.scalar.dma_start(w1_sb[:], w1)
        table_blocks = table.rearrange("(b p) d -> p b d", p=P)
        rows = []
        for piece in range(PIECES):
            rows_piece = held.tile([P, PIECE_BLOCKS, P], BF16, name=f"rows{piece}")
            nc.sync.dma_start(
                rows_piece[:],
                table_blocks[:, piece * PIECE_BLOCKS : (piece + 1) * PIECE_BLOCKS, :],
            )
            rows.append(rows_piece)
        offsets = held.tile([P, CELLS // 16], U16, name="offsets")
        nc.sync.dma_start(offsets[:], offs)
        scale_sb = held.tile([P, 1], F32, name="scale_sb")
        bias_sb = held.tile([P, 1], F32, name="bias_sb")
        w4_sb = held.tile([P, P], BF16, name="w4_sb")
        b4_sb = held.tile([P, 1], F32, name="b4_sb")
        with nc.allow_non_contiguous_dma(reason="one float to a partition"):
            nc.sync.dma_start(scale_sb[:], ln_scale)
            nc.sync.dma_start(bias_sb[:], ln_bias)
            nc.sync.dma_start(w4_sb[:], w4)
            nc.sync.dma_start(b4_sb[:], b4)

        ident_bf = held.tile([P, P], BF16, name="ident_bf")
        make_identity(nc, ident_bf[:])
        mean_weights = held.tile([P, P], F32, name="mean_weights")
        nc.vector.memset(mean_weights[:], 1.0 / P)
        eps = held.tile([P, 1], F32, name="eps")
        nc.vector.memset(eps[:], LN_EPS)
        warm = held.tile([P, 1], F32, name="warm")
        nc.scalar.activation(warm[:], eps[:], ACT.Abs_reciprocal_sqrt)

        b1_mean_ps = chain.tile([P, 1], F32, name="b1_mean_ps")
        nc.tensor.matmul(b1_mean_ps[:], mean_weights[:], b1_sb[:], start=True, stop=True)
        b1c = held.tile([P, 1], F32, name="b1c")
        nc.vector.tensor_tensor(b1c[:], b1_sb[:], b1_mean_ps[:], ALU.subtract)
        w1_over_p = held.tile([P, P], F32, name="w1_over_p")
        w1_mean = held.tile([P, 1], F32, name="w1_mean")
        nc.scalar.activation(w1_over_p[:], w1_sb[:], ACT.Copy, scale=1.0 / P, accum_out=w1_mean[:])
        w1c_hi = held.tile([P, P], BF16, name="w1c_hi")
        nc.vector.tensor_scalar_sub(w1c_hi[:], w1_sb[:], w1_mean[:])
        w1c_lo = held.tile([P, P], BF16, name="w1c_lo")
        nc.vector.scalar_tensor_tensor(
            w1c_lo[:], w1_sb[:], w1_mean[:], w1c_hi[:], ALU.subtract, ALU.subtract
        )

        window = held.tile([P, GENES], BF16, name="window")
        for piece in range(PIECES):
            flipped = flip.tile([P, PIECE_GENES], BF16, name="flipped")
            for block in range(PIECE_BLOCKS):
                nc.tensor.transpose(
                    flipped[:, block * P : (block + 1) * P], rows[piece][:, block, :], ident_bf[:]
                )
            window_part = window[:, piece * PIECE_GENES : (piece + 1) * PIECE_GENES]
            if piece % 2 == 0:
                nc.vector.tensor_copy(window_part, flipped[:])
            else:
                nc.scalar.copy(window_part, flipped[:])

        uc_ps = chain.tile([P, CELLS], F32, name="uc_ps")
        nc.tensor.matmul(uc_ps[:], w1c_hi[:], window[:].indirect(offsets[:]), start=True, stop=False)
        nc.tensor.matmul(uc_ps[:], w1c_lo[:], window[:].indirect(offsets[:]), start=False, stop=True)

        squares = held.tile([P, CELLS], F32, name="squares")
        nc.scalar.activation(squares[:], uc_ps[:], ACT.Square, bias=b1c[:])
        var_ps = chain.tile([P, CELLS], F32, name="var_ps")
        nc.tensor.matmul(var_ps[:], mean_weights[:], squares[:], start=True, stop=True)
        gained = held.tile([P, CELLS], F32, name="gained")
        nc.vector.tensor_scalar(gained[:], uc_ps[:], b1c[:], scale_sb[:], ALU.add, ALU.mult)
        rstd = held.tile([P, CELLS], F32, name="rstd")
        nc.scalar.activation(rstd[:], var_ps[:], ACT.Abs_reciprocal_sqrt, bias=eps[:])

        normed = held.tile([P, CELLS], F32, name="normed")
        nc.vector.tensor_tensor(normed[:], gained[:], rstd[:], ALU.mult)
        h = held.tile([P, CELLS], BF16, name="h")
        nc.vector.tensor_scalar(h[:], normed[:], bias_sb[:], 0.0, ALU.add, ALU.max)

        o_ps = chain.tile([P, CELLS], F32, name="o_ps")
        nc.tensor.matmul(o_ps[:], w4_sb[:], h[:], start=True, stop=True)
        result = held.tile([P, CELLS], F32, name="result")
        nc.scalar.activation(result[:], o_ps[:], ACT.Exp, bias=b4_sb[:])
        nc.sync.dma_start(out, result[:])
